import numpy as np
import ml_dtypes

BF16 = ml_dtypes.bfloat16


def bf(x):
    return np.asarray(x, np.float32).astype(BF16)


def f32(x):
    return np.asarray(x, np.float32)


def f64(x):
    return np.asarray(x).astype(np.float64)


def striped(idx):
    return np.tile(idx.reshape(-1, 16).T, (8, 1))


D, HEADS, S, N = 128, 2, 2048, 2048
EPS = 1e-5


def setup_inputs():
    return {
        "x": bf(np.random.standard_normal((D, S))),
        "wv": bf(np.random.standard_normal((D, HEADS * D)) / np.sqrt(D)),
        "bv": f32(0.1 * np.random.standard_normal((HEADS * D, 1))),
        "wskip": bf(np.random.standard_normal((D, D)) / np.sqrt(D)),
        "bskip": f32(0.1 * np.random.standard_normal((D, 1))),
        "gamma": f32(1.0 + 0.1 * np.random.standard_normal((D, 1))),
        "beta": f32(0.1 * np.random.standard_normal((D, 1))),
        "offs": striped(np.random.permutation(np.tile(np.arange(S), 2))[:N]),
    }


def reference(x, wv, bv, wskip, bskip, gamma, beta, offs):
    idx = offs[:16].T.reshape(-1)
    xs = f64(x)
    val = f64(wv).T @ xs[:, idx] + f64(bv)
    agg = val.reshape(HEADS, D, N).mean(axis=0)
    t = agg + f64(wskip).T @ xs + f64(bskip)
    mu = t.mean(axis=0, keepdims=True)
    var = ((t - mu) ** 2).mean(axis=0, keepdims=True)
    return (t - mu) / np.sqrt(var + EPS) * f64(gamma) + f64(beta) + xs

@@ -1,0 +1,110 @@
+import concourse.mybir as mybir
+from concourse.masks import make_identity
+
+BF16, F32, U16 = mybir.dt.bfloat16, mybir.dt.float32, mybir.dt.uint16
+ACT = mybir.ActivationFunctionType
+ALU = mybir.AluOpType
+
+P = 128
+HEADS = 2
+NODES = 2048
+PIECE = 512
+PIECES = NODES // PIECE
+BLOCKS = PIECE // P
+EPS = 1e-5
+
+FLOPS = 2 * P * (HEADS * P + P) * NODES
+
+
+def tile_graphtransformer_kernel(tc, x, wv, bv, wskip, bskip, gamma, beta, offs, out):
+    nc = tc.nc
+    with (
+        tc.tile_pool(name="held", bufs=1) as held,
+        tc.tile_pool(name="work", bufs=2) as work,
+        tc.psum_pool(name="sums", bufs=PIECES) as sums,
+        tc.psum_pool(name="turned", bufs=2) as turned,
+    ):
+        offsets = held.tile([P, NODES // 16], U16, name="offsets")
+        nc.sync.dma_start(offsets[:], offs)
+        wv_sb = held.tile([P, HEADS * P], BF16, name="wv_sb")
+        nc.sync.dma_start(wv_sb[:], wv)
+        wskip_sb = held.tile([P, P], BF16, name="wskip_sb")
+        nc.scalar.dma_start(wskip_sb[:], wskip)
+        x_sb = held.tile([P, NODES], BF16, name="x_sb")
+        for p in range(PIECES):
+            cols = slice(p * PIECE, (p + 1) * PIECE)
+            queue = nc.sync if p % 2 == 0 else nc.scalar
+            queue.dma_start(x_sb[:, cols], x[:, cols])
+
+        rows = held.tile([P, P], F32, name="rows")
+        nc.vector.memset(rows[:], 0.0)
+        nc.gpsimd.dma_start(rows[0:2, :], bv.rearrange("(h c) o -> (h o) c", h=HEADS))
+        nc.gpsimd.dma_start(rows[2:3, :], bskip.rearrange("c o -> o c"))
+        nc.gpsimd.dma_start(rows[3:4, :], gamma.rearrange("c o -> o c"))
+        nc.gpsimd.dma_start(rows[4:5, :], beta.rearrange("c o -> o c"))
+
+        identity = held.tile([P, P], F32, name="identity")
+        make_identity(nc, identity[:])
+        eps = held.tile([P, 1], F32, name="eps")
+        nc.vector.memset(eps[:], EPS)
+
+        columns_ps = turned.tile([P, P], F32, name="columns_ps", tag="by_node")
+        nc.tensor.transpose(columns_ps[:], rows[:], identity[:])
+        columns = held.tile([P, 5], F32, name="columns")
+        nc.vector.tensor_copy(columns[:], columns_ps[:, 0:5])
+        gamma_col, beta_col = columns[:, 3:4], columns[:, 4:5]
+        bv_sum = held.tile([P, 1], F32, name="bv_sum")
+        nc.vector.tensor_tensor(bv_sum[:], columns[:, 0:1], columns[:, 1:2], ALU.add)
+        bias = held.tile([P, 1], F32, name="bias")
+        nc.vector.scalar_tensor_tensor(bias[:], bv_sum[:], 0.5, columns[:, 2:3], ALU.mult, ALU.add)
+
+        wv_half = held.tile([P, HEADS * P], BF16, name="wv_half")
+        nc.vector.tensor_scalar(wv_half[:], wv_sb[:], 0.5, None, ALU.mult)
+
+        t_ps = [sums.tile([P, PIECE], F32, name="t_ps") for p in range(PIECES)]
+        for p in range(PIECES):
+            nc.tensor.matmul(t_ps[p][:], wskip_sb[:], x_sb[:, p * PIECE : (p + 1) * PIECE], start=True, stop=False)
+        for p in range(PIECES):
+            picked = x_sb[:].indirect(offsets[:, p * (PIECE // 16) : (p + 1) * (PIECE // 16)])
+            nc.tensor.matmul(t_ps[p][:], wv_half[:, 0:P], picked, start=False, stop=False)
+            nc.tensor.matmul(t_ps[p][:], wv_half[:, P : 2 * P], picked, start=False, stop=True)
+
+        x_beta = held.tile([P, NODES], F32, name="x_beta")
+        for p in range(PIECES):
+            cols = slice(p * PIECE, (p + 1) * PIECE)
+            nc.gpsimd.tensor_scalar(x_beta[:, cols], x_sb[:, cols], 1.0, beta_col, ALU.mult, ALU.add)
+
+        for p in range(PIECES):
+            cols = slice(p * PIECE, (p + 1) * PIECE)
+            t = work.tile([P, PIECE], F32, name="t")
+            nc.scalar.activation(t[:], t_ps[p][:], ACT.Identity, bias=bias[:])
+
+            by_node = turned.tile([P, BLOCKS, P], F32, name="by_node")
+            for b in range(BLOCKS):
+                nc.tensor.transpose(by_node[:, b, :], t[:, b * P : (b + 1) * P], identity[:])
+
+            stats = work.tile([P, BLOCKS, 6], F32, name="stats")
+            mean_var = work.tile([P, BLOCKS, 2], F32, name="mean_var")
+            for b in range(BLOCKS):
+                nc.vector.bn_stats(stats[:, b, :], by_node[:, b, :])
+                nc.vector.bn_aggr(mean_var[:, b, :], stats[:, b, :])
+            std = work.tile([P, BLOCKS], F32, name="std")
+            nc.scalar.activation(std[:], mean_var[:, :, 1], ACT.Sqrt, bias=eps[:])
+            rstd = work.tile([P, BLOCKS], F32, name="rstd")
+            nc.vector.reciprocal(rstd[:], std[:])
+            shift = work.tile([P, BLOCKS], F32, name="shift")
+            nc.vector.scalar_tensor_tensor(shift[:], mean_var[:, :, 0], -1.0, rstd[:], ALU.mult, ALU.mult)
+
+            normed = work.tile([P, BLOCKS, P], F32, name="normed")
+            for b in range(BLOCKS):
+                nc.scalar.activation(
+                    normed[:, b, :], by_node[:, b, :], ACT.Identity, bias=shift[:, b : b + 1], scale=rstd[:, b : b + 1]
+                )
+
+            by_channel = turned.tile([P, PIECE], F32, name="by_channel")
+            for b in range(BLOCKS):
+                nc.tensor.transpose(by_channel[:, b * P : (b + 1) * P], normed[:, b, :], identity[:])
+
+            result = work.tile([P, PIECE], F32, name="result")
+            nc.vector.scalar_tensor_tensor(result[:], by_channel[:], gamma_col, x_beta[:, cols], ALU.mult, ALU.add)
+            nc.sync.dma_start(out[:, cols], result[:])

@@ -11,6 +11,7 @@ NODES = 2048
 PIECE = 512
 PIECES = NODES // PIECE
 BLOCKS = PIECE // P
+PSUM_BANKS = 8
 EPS = 1e-5
 
 FLOPS = 2 * P * (HEADS * P + P) * NODES
@@ -18,38 +19,50 @@ FLOPS = 2 * P * (HEADS * P + P) * NODES
 
 def tile_graphtransformer_kernel(tc, x, wv, bv, wskip, bskip, gamma, beta, offs, out):
     nc = tc.nc
+    pieces = [slice(p * PIECE, (p + 1) * PIECE) for p in range(PIECES)]
     with (
         tc.tile_pool(name="held", bufs=1) as held,
-        tc.tile_pool(name="work", bufs=2) as work,
-        tc.psum_pool(name="sums", bufs=PIECES) as sums,
-        tc.psum_pool(name="turned", bufs=2) as turned,
+        tc.tile_pool(name="work", bufs=PIECES) as work,
+        tc.psum_pool(name="psum", bufs=PSUM_BANKS) as psum,
     ):
         offsets = held.tile([P, NODES // 16], U16, name="offsets")
-        nc.sync.dma_start(offsets[:], offs)
         wv_sb = held.tile([P, HEADS * P], BF16, name="wv_sb")
-        nc.sync.dma_start(wv_sb[:], wv)
         wskip_sb = held.tile([P, P], BF16, name="wskip_sb")
-        nc.scalar.dma_start(wskip_sb[:], wskip)
         x_sb = held.tile([P, NODES], BF16, name="x_sb")
+        nc.sync.dma_start(offsets[:], offs)
+        nc.scalar.dma_start(wskip_sb[:], wskip)
+        nc.scalar.dma_start(wv_sb[:], wv)
         for p in range(PIECES):
-            cols = slice(p * PIECE, (p + 1) * PIECE)
             queue = nc.sync if p % 2 == 0 else nc.scalar
-            queue.dma_start(x_sb[:, cols], x[:, cols])
+            queue.dma_start(x_sb[:, pieces[p]], x[:, pieces[p]])
 
         rows = held.tile([P, P], F32, name="rows")
         nc.vector.memset(rows[:], 0.0)
-        nc.gpsimd.dma_start(rows[0:2, :], bv.rearrange("(h c) o -> (h o) c", h=HEADS))
-        nc.gpsimd.dma_start(rows[2:3, :], bskip.rearrange("c o -> o c"))
-        nc.gpsimd.dma_start(rows[3:4, :], gamma.rearrange("c o -> o c"))
-        nc.gpsimd.dma_start(rows[4:5, :], beta.rearrange("c o -> o c"))
+        nc.sync.dma_start(rows[0:2, :], bv.rearrange("(h c) o -> (h o) c", h=HEADS))
+        nc.scalar.dma_start(rows[2:3, :], bskip.rearrange("c o -> o c"))
+        nc.sync.dma_start(rows[3:4, :], gamma.rearrange("c o -> o c"))
+        nc.scalar.dma_start(rows[4:5, :], beta.rearrange("c o -> o c"))
 
         identity = held.tile([P, P], F32, name="identity")
         make_identity(nc, identity[:])
         eps = held.tile([P, 1], F32, name="eps")
         nc.vector.memset(eps[:], EPS)
 
-        columns_ps = turned.tile([P, P], F32, name="columns_ps", tag="by_node")
+        wv_half = held.tile([P, HEADS * P], BF16, name="wv_half")
+        nc.vector.tensor_scalar(wv_half[:], wv_sb[:], 0.5, None, ALU.mult)
+
+        t_ps = [psum.tile([P, PIECE], F32, name="t_ps", tag="bank") for p in range(PIECES)]
+        for p in range(PIECES):
+            nc.tensor.matmul(t_ps[p][:], wskip_sb[:], x_sb[:, pieces[p]], start=True, stop=False)
+
+        columns_ps = psum.tile([P, P], F32, name="columns_ps", tag="bank")
         nc.tensor.transpose(columns_ps[:], rows[:], identity[:])
+
+        for p in range(PIECES):
+            picked = x_sb[:].indirect(offsets[:, p * (PIECE // 16) : (p + 1) * (PIECE // 16)])
+            nc.tensor.matmul(t_ps[p][:], wv_half[:, 0:P], picked, start=False, stop=False)
+            nc.tensor.matmul(t_ps[p][:], wv_half[:, P : 2 * P], picked, start=False, stop=True)
+
         columns = held.tile([P, 5], F32, name="columns")
         nc.vector.tensor_copy(columns[:], columns_ps[:, 0:5])
         gamma_col, beta_col = columns[:, 3:4], columns[:, 4:5]
@@ -58,35 +71,24 @@ def tile_graphtransformer_kernel(tc, x, wv, bv, wskip, bskip, gamma, beta, offs,
         bias = held.tile([P, 1], F32, name="bias")
         nc.vector.scalar_tensor_tensor(bias[:], bv_sum[:], 0.5, columns[:, 2:3], ALU.mult, ALU.add)
 
-        wv_half = held.tile([P, HEADS * P], BF16, name="wv_half")
-        nc.vector.tensor_scalar(wv_half[:], wv_sb[:], 0.5, None, ALU.mult)
-
-        t_ps = [sums.tile([P, PIECE], F32, name="t_ps") for p in range(PIECES)]
-        for p in range(PIECES):
-            nc.tensor.matmul(t_ps[p][:], wskip_sb[:], x_sb[:, p * PIECE : (p + 1) * PIECE], start=True, stop=False)
-        for p in range(PIECES):
-            picked = x_sb[:].indirect(offsets[:, p * (PIECE // 16) : (p + 1) * (PIECE // 16)])
-            nc.tensor.matmul(t_ps[p][:], wv_half[:, 0:P], picked, start=False, stop=False)
-            nc.tensor.matmul(t_ps[p][:], wv_half[:, P : 2 * P], picked, start=False, stop=True)
-
         x_beta = held.tile([P, NODES], F32, name="x_beta")
         for p in range(PIECES):
-            cols = slice(p * PIECE, (p + 1) * PIECE)
-            nc.gpsimd.tensor_scalar(x_beta[:, cols], x_sb[:, cols], 1.0, beta_col, ALU.mult, ALU.add)
+            nc.gpsimd.tensor_scalar(x_beta[:, pieces[p]], x_sb[:, pieces[p]], 1.0, beta_col, ALU.mult, ALU.add)
 
+        by_node = []
         for p in range(PIECES):
-            cols = slice(p * PIECE, (p + 1) * PIECE)
             t = work.tile([P, PIECE], F32, name="t")
             nc.scalar.activation(t[:], t_ps[p][:], ACT.Identity, bias=bias[:])
-
-            by_node = turned.tile([P, BLOCKS, P], F32, name="by_node")
+            by_node.append(psum.tile([P, BLOCKS, P], F32, name="by_node", tag="bank"))
             for b in range(BLOCKS):
-                nc.tensor.transpose(by_node[:, b, :], t[:, b * P : (b + 1) * P], identity[:])
+                nc.tensor.transpose(by_node[p][:, b, :], t[:, b * P : (b + 1) * P], identity[:])
 
+        normed = []
+        for p in range(PIECES):
             stats = work.tile([P, BLOCKS, 6], F32, name="stats")
             mean_var = work.tile([P, BLOCKS, 2], F32, name="mean_var")
             for b in range(BLOCKS):
-                nc.vector.bn_stats(stats[:, b, :], by_node[:, b, :])
+                nc.vector.bn_stats(stats[:, b, :], by_node[p][:, b, :])
                 nc.vector.bn_aggr(mean_var[:, b, :], stats[:, b, :])
             std = work.tile([P, BLOCKS], F32, name="std")
             nc.scalar.activation(std[:], mean_var[:, :, 1], ACT.Sqrt, bias=eps[:])
@@ -94,17 +96,16 @@ def tile_graphtransformer_kernel(tc, x, wv, bv, wskip, bskip, gamma, beta, offs,
             nc.vector.reciprocal(rstd[:], std[:])
             shift = work.tile([P, BLOCKS], F32, name="shift")
             nc.vector.scalar_tensor_tensor(shift[:], mean_var[:, :, 0], -1.0, rstd[:], ALU.mult, ALU.mult)
-
-            normed = work.tile([P, BLOCKS, P], F32, name="normed")
+            normed.append(work.tile([P, BLOCKS, P], F32, name="normed"))
             for b in range(BLOCKS):
                 nc.scalar.activation(
-                    normed[:, b, :], by_node[:, b, :], ACT.Identity, bias=shift[:, b : b + 1], scale=rstd[:, b : b + 1]
+                    normed[p][:, b, :], by_node[p][:, b, :], ACT.Identity, bias=shift[:, b : b + 1], scale=rstd[:, b : b + 1]
                 )
 
-            by_channel = turned.tile([P, PIECE], F32, name="by_channel")
+        for p in range(PIECES):
+            by_channel = psum.tile([P, PIECE], F32, name="by_channel", tag="bank")
             for b in range(BLOCKS):
-                nc.tensor.transpose(by_channel[:, b * P : (b + 1) * P], normed[:, b, :], identity[:])
-
+                nc.tensor.transpose(by_channel[:, b * P : (b + 1) * P], normed[p][:, b, :], identity[:])
             result = work.tile([P, PIECE], F32, name="result")
-            nc.vector.scalar_tensor_tensor(result[:], by_channel[:], gamma_col, x_beta[:, cols], ALU.mult, ALU.add)
-            nc.sync.dma_start(out[:, cols], result[:])
+            nc.vector.scalar_tensor_tensor(result[:], by_channel[:], gamma_col, x_beta[:, pieces[p]], ALU.mult, ALU.add)
+            nc.sync.dma_start(out[:, pieces[p]], result[:])

@@ -12,6 +12,7 @@ PIECE = 512
 PIECES = NODES // PIECE
 BLOCKS = PIECE // P
 PSUM_BANKS = 8
+WARM_UP = 3
 EPS = 1e-5
 
 FLOPS = 2 * P * (HEADS * P + P) * NODES
@@ -25,6 +26,19 @@ def tile_graphtransformer_kernel(tc, x, wv, bv, wskip, bskip, gamma, beta, offs,
         tc.tile_pool(name="work", bufs=PIECES) as work,
         tc.psum_pool(name="psum", bufs=PSUM_BANKS) as psum,
     ):
+        zeros = held.tile([P, PIECE], BF16, name="zeros")
+        nc.vector.memset(zeros[:], 0.0)
+        unread_ps = psum.tile([P, PIECE], F32, name="unread_ps", tag="bank")
+        for w in range(WARM_UP):
+            nc.tensor.matmul(unread_ps[:], zeros[:, 0:P], zeros[:], start=True, stop=True)
+
+        rows = held.tile([P, P], F32, name="rows")
+        nc.gpsimd.memset(rows[:], 0.0)
+        nc.sync.dma_start(rows[0:2, :], bv.rearrange("(h c) o -> (h o) c", h=HEADS))
+        nc.scalar.dma_start(rows[2:3, :], bskip.rearrange("c o -> o c"))
+        nc.sync.dma_start(rows[3:4, :], gamma.rearrange("c o -> o c"))
+        nc.scalar.dma_start(rows[4:5, :], beta.rearrange("c o -> o c"))
+
         offsets = held.tile([P, NODES // 16], U16, name="offsets")
         wv_sb = held.tile([P, HEADS * P], BF16, name="wv_sb")
         wskip_sb = held.tile([P, P], BF16, name="wskip_sb")
@@ -36,17 +50,20 @@ def tile_graphtransformer_kernel(tc, x, wv, bv, wskip, bskip, gamma, beta, offs,
             queue = nc.sync if p % 2 == 0 else nc.scalar
             queue.dma_start(x_sb[:, pieces[p]], x[:, pieces[p]])
 
-        rows = held.tile([P, P], F32, name="rows")
-        nc.vector.memset(rows[:], 0.0)
-        nc.sync.dma_start(rows[0:2, :], bv.rearrange("(h c) o -> (h o) c", h=HEADS))
-        nc.scalar.dma_start(rows[2:3, :], bskip.rearrange("c o -> o c"))
-        nc.sync.dma_start(rows[3:4, :], gamma.rearrange("c o -> o c"))
-        nc.scalar.dma_start(rows[4:5, :], beta.rearrange("c o -> o c"))
-
         identity = held.tile([P, P], F32, name="identity")
         make_identity(nc, identity[:])
         eps = held.tile([P, 1], F32, name="eps")
         nc.vector.memset(eps[:], EPS)
+
+        columns_ps = psum.tile([P, P], F32, name="columns_ps", tag="bank")
+        nc.tensor.transpose(columns_ps[:], rows[:], identity[:])
+        columns = held.tile([P, 5], F32, name="columns")
+        nc.vector.tensor_copy(columns[:], columns_ps[:, 0:5])
+        gamma_col, beta_col = columns[:, 3:4], columns[:, 4:5]
+        bv_sum = held.tile([P, 1], F32, name="bv_sum")
+        nc.vector.tensor_tensor(bv_sum[:], columns[:, 0:1], columns[:, 1:2], ALU.add)
+        bias = held.tile([P, 1], F32, name="bias")
+        nc.vector.scalar_tensor_tensor(bias[:], bv_sum[:], 0.5, columns[:, 2:3], ALU.mult, ALU.add)
 
         wv_half = held.tile([P, HEADS * P], BF16, name="wv_half")
         nc.vector.tensor_scalar(wv_half[:], wv_sb[:], 0.5, None, ALU.mult)
@@ -55,21 +72,10 @@ def tile_graphtransformer_kernel(tc, x, wv, bv, wskip, bskip, gamma, beta, offs,
         for p in range(PIECES):
             nc.tensor.matmul(t_ps[p][:], wskip_sb[:], x_sb[:, pieces[p]], start=True, stop=False)
 
-        columns_ps = psum.tile([P, P], F32, name="columns_ps", tag="bank")
-        nc.tensor.transpose(columns_ps[:], rows[:], identity[:])
-
         for p in range(PIECES):
             picked = x_sb[:].indirect(offsets[:, p * (PIECE // 16) : (p + 1) * (PIECE // 16)])
             nc.tensor.matmul(t_ps[p][:], wv_half[:, 0:P], picked, start=False, stop=False)
             nc.tensor.matmul(t_ps[p][:], wv_half[:, P : 2 * P], picked, start=False, stop=True)
-
-        columns = held.tile([P, 5], F32, name="columns")
-        nc.vector.tensor_copy(columns[:], columns_ps[:, 0:5])
-        gamma_col, beta_col = columns[:, 3:4], columns[:, 4:5]
-        bv_sum = held.tile([P, 1], F32, name="bv_sum")
-        nc.vector.tensor_tensor(bv_sum[:], columns[:, 0:1], columns[:, 1:2], ALU.add)
-        bias = held.tile([P, 1], F32, name="bias")
-        nc.vector.scalar_tensor_tensor(bias[:], bv_sum[:], 0.5, columns[:, 2:3], ALU.mult, ALU.add)
 
         x_beta = held.tile([P, NODES], F32, name="x_beta")
         for p in range(PIECES):
@@ -90,10 +96,8 @@ def tile_graphtransformer_kernel(tc, x, wv, bv, wskip, bskip, gamma, beta, offs,
             for b in range(BLOCKS):
                 nc.vector.bn_stats(stats[:, b, :], by_node[p][:, b, :])
                 nc.vector.bn_aggr(mean_var[:, b, :], stats[:, b, :])
-            std = work.tile([P, BLOCKS], F32, name="std")
-            nc.scalar.activation(std[:], mean_var[:, :, 1], ACT.Sqrt, bias=eps[:])
             rstd = work.tile([P, BLOCKS], F32, name="rstd")
-            nc.vector.reciprocal(rstd[:], std[:])
+            nc.scalar.activation(rstd[:], mean_var[:, :, 1], ACT.Abs_reciprocal_sqrt, bias=eps[:])
             shift = work.tile([P, BLOCKS], F32, name="shift")
             nc.vector.scalar_tensor_tensor(shift[:], mean_var[:, :, 0], -1.0, rstd[:], ALU.mult, ALU.mult)
             normed.append(work.tile([P, BLOCKS, P], F32, name="normed"))

@@ -10,7 +10,9 @@ HEADS = 2
 NODES = 2048
 PIECE = 512
 PIECES = NODES // PIECE
-BLOCKS = PIECE // P
+UNIT = 256
+UNITS = NODES // UNIT
+BLOCKS = UNIT // P
 PSUM_BANKS = 8
 WARM_UP = 3
 EPS = 1e-5
@@ -21,9 +23,10 @@ FLOPS = 2 * P * (HEADS * P + P) * NODES
 def tile_graphtransformer_kernel(tc, x, wv, bv, wskip, bskip, gamma, beta, offs, out):
     nc = tc.nc
     pieces = [slice(p * PIECE, (p + 1) * PIECE) for p in range(PIECES)]
+    units = [slice(u * UNIT, (u + 1) * UNIT) for u in range(UNITS)]
     with (
         tc.tile_pool(name="held", bufs=1) as held,
-        tc.tile_pool(name="work", bufs=PIECES) as work,
+        tc.tile_pool(name="work", bufs=UNITS) as work,
         tc.psum_pool(name="psum", bufs=PSUM_BANKS) as psum,
     ):
         zeros = held.tile([P, PIECE], BF16, name="zeros")
@@ -82,19 +85,20 @@ def tile_graphtransformer_kernel(tc, x, wv, bv, wskip, bskip, gamma, beta, offs,
             nc.gpsimd.tensor_scalar(x_beta[:, pieces[p]], x_sb[:, pieces[p]], 1.0, beta_col, ALU.mult, ALU.add)
 
         by_node = []
-        for p in range(PIECES):
-            t = work.tile([P, PIECE], F32, name="t")
-            nc.scalar.activation(t[:], t_ps[p][:], ACT.Identity, bias=bias[:])
+        for u in range(UNITS):
+            t = work.tile([P, UNIT], F32, name="t")
+            in_piece = slice((u * UNIT) % PIECE, (u * UNIT) % PIECE + UNIT)
+            nc.scalar.activation(t[:], t_ps[u * UNIT // PIECE][:, in_piece], ACT.Identity, bias=bias[:])
             by_node.append(psum.tile([P, BLOCKS, P], F32, name="by_node", tag="bank"))
             for b in range(BLOCKS):
-                nc.tensor.transpose(by_node[p][:, b, :], t[:, b * P : (b + 1) * P], identity[:])
+                nc.tensor.transpose(by_node[u][:, b, :], t[:, b * P : (b + 1) * P], identity[:])
 
         normed = []
-        for p in range(PIECES):
+        for u in range(UNITS):
             stats = work.tile([P, BLOCKS, 6], F32, name="stats")
             mean_var = work.tile([P, BLOCKS, 2], F32, name="mean_var")
             for b in range(BLOCKS):
-                nc.vector.bn_stats(stats[:, b, :], by_node[p][:, b, :])
+                nc.vector.bn_stats(stats[:, b, :], by_node[u][:, b, :])
                 nc.vector.bn_aggr(mean_var[:, b, :], stats[:, b, :])
             rstd = work.tile([P, BLOCKS], F32, name="rstd")
             nc.scalar.activation(rstd[:], mean_var[:, :, 1], ACT.Abs_reciprocal_sqrt, bias=eps[:])
@@ -103,13 +107,13 @@ def tile_graphtransformer_kernel(tc, x, wv, bv, wskip, bskip, gamma, beta, offs,
             normed.append(work.tile([P, BLOCKS, P], F32, name="normed"))
             for b in range(BLOCKS):
                 nc.scalar.activation(
-                    normed[p][:, b, :], by_node[p][:, b, :], ACT.Identity, bias=shift[:, b : b + 1], scale=rstd[:, b : b + 1]
+                    normed[u][:, b, :], by_node[u][:, b, :], ACT.Identity, bias=shift[:, b : b + 1], scale=rstd[:, b : b + 1]
                 )
 
-        for p in range(PIECES):
-            by_channel = psum.tile([P, PIECE], F32, name="by_channel", tag="bank")
+        for u in range(UNITS):
+            by_channel = psum.tile([P, UNIT], F32, name="by_channel", tag="bank")
             for b in range(BLOCKS):
-                nc.tensor.transpose(by_channel[:, b * P : (b + 1) * P], normed[p][:, b, :], identity[:])
-            result = work.tile([P, PIECE], F32, name="result")
-            nc.vector.scalar_tensor_tensor(result[:], by_channel[:], gamma_col, x_beta[:, pieces[p]], ALU.mult, ALU.add)
-            nc.sync.dma_start(out[:, pieces[p]], result[:])
+                nc.tensor.transpose(by_channel[:, b * P : (b + 1) * P], normed[u][:, b, :], identity[:])
+            result = work.tile([P, UNIT], F32, name="result")
+            nc.vector.scalar_tensor_tensor(result[:], by_channel[:], gamma_col, x_beta[:, units[u]], ALU.mult, ALU.add)
+            nc.sync.dma_start(out[:, units[u]], result[:])

@@ -10,9 +10,7 @@ HEADS = 2
 NODES = 2048
 PIECE = 512
 PIECES = NODES // PIECE
-UNIT = 256
-UNITS = NODES // UNIT
-BLOCKS = UNIT // P
+BLOCKS = PIECE // P
 PSUM_BANKS = 8
 WARM_UP = 3
 EPS = 1e-5
@@ -23,10 +21,9 @@ FLOPS = 2 * P * (HEADS * P + P) * NODES
 def tile_graphtransformer_kernel(tc, x, wv, bv, wskip, bskip, gamma, beta, offs, out):
     nc = tc.nc
     pieces = [slice(p * PIECE, (p + 1) * PIECE) for p in range(PIECES)]
-    units = [slice(u * UNIT, (u + 1) * UNIT) for u in range(UNITS)]
     with (
         tc.tile_pool(name="held", bufs=1) as held,
-        tc.tile_pool(name="work", bufs=UNITS) as work,
+        tc.tile_pool(name="work", bufs=PIECES) as work,
         tc.psum_pool(name="psum", bufs=PSUM_BANKS) as psum,
     ):
         zeros = held.tile([P, PIECE], BF16, name="zeros")
@@ -85,35 +82,36 @@ def tile_graphtransformer_kernel(tc, x, wv, bv, wskip, bskip, gamma, beta, offs,
             nc.gpsimd.tensor_scalar(x_beta[:, pieces[p]], x_sb[:, pieces[p]], 1.0, beta_col, ALU.mult, ALU.add)
 
         by_node = []
-        for u in range(UNITS):
-            t = work.tile([P, UNIT], F32, name="t")
-            in_piece = slice((u * UNIT) % PIECE, (u * UNIT) % PIECE + UNIT)
-            nc.scalar.activation(t[:], t_ps[u * UNIT // PIECE][:, in_piece], ACT.Identity, bias=bias[:])
+        for p in range(PIECES):
+            t = work.tile([P, PIECE], F32, name="t")
+            nc.scalar.activation(t[:], t_ps[p][:], ACT.Identity, bias=bias[:])
             by_node.append(psum.tile([P, BLOCKS, P], F32, name="by_node", tag="bank"))
             for b in range(BLOCKS):
-                nc.tensor.transpose(by_node[u][:, b, :], t[:, b * P : (b + 1) * P], identity[:])
+                nc.tensor.transpose(by_node[p][:, b, :], t[:, b * P : (b + 1) * P], identity[:])
 
         normed = []
-        for u in range(UNITS):
-            stats = work.tile([P, BLOCKS, 6], F32, name="stats")
-            mean_var = work.tile([P, BLOCKS, 2], F32, name="mean_var")
-            for b in range(BLOCKS):
-                nc.vector.bn_stats(stats[:, b, :], by_node[u][:, b, :])
-                nc.vector.bn_aggr(mean_var[:, b, :], stats[:, b, :])
+        for p in range(PIECES):
+            stats = work.tile([P, BLOCKS, 3], F32, name="stats")
+            for b in range(0, BLOCKS, 2):
+                nc.vector.bn_stats(
+                    stats[:, b : b + 2, :].rearrange("j b s -> j (b s)"),
+                    by_node[p][:, b : b + 2, :].rearrange("j b c -> j c b"),
+                )
+            mean, var_times_p = stats[:, :, 1], stats[:, :, 2]
             rstd = work.tile([P, BLOCKS], F32, name="rstd")
-            nc.scalar.activation(rstd[:], mean_var[:, :, 1], ACT.Abs_reciprocal_sqrt, bias=eps[:])
+            nc.scalar.activation(rstd[:], var_times_p, ACT.Abs_reciprocal_sqrt, bias=eps[:], scale=1.0 / P)
             shift = work.tile([P, BLOCKS], F32, name="shift")
-            nc.vector.scalar_tensor_tensor(shift[:], mean_var[:, :, 0], -1.0, rstd[:], ALU.mult, ALU.mult)
+            nc.vector.scalar_tensor_tensor(shift[:], mean, -1.0, rstd[:], ALU.mult, ALU.mult)
             normed.append(work.tile([P, BLOCKS, P], F32, name="normed"))
             for b in range(BLOCKS):
                 nc.scalar.activation(
-                    normed[u][:, b, :], by_node[u][:, b, :], ACT.Identity, bias=shift[:, b : b + 1], scale=rstd[:, b : b + 1]
+                    normed[p][:, b, :], by_node[p][:, b, :], ACT.Identity, bias=shift[:, b : b + 1], scale=rstd[:, b : b + 1]
                 )
 
-        for u in range(UNITS):
-            by_channel = psum.tile([P, UNIT], F32, name="by_channel", tag="bank")
+        for p in range(PIECES):
+            by_channel = psum.tile([P, PIECE], F32, name="by_channel", tag="bank")
             for b in range(BLOCKS):
-                nc.tensor.transpose(by_channel[:, b * P : (b + 1) * P], normed[u][:, b, :], identity[:])
-            result = work.tile([P, UNIT], F32, name="result")
-            nc.vector.scalar_tensor_tensor(result[:], by_channel[:], gamma_col, x_beta[:, units[u]], ALU.mult, ALU.add)
-            nc.sync.dma_start(out[:, units[u]], result[:])
+                nc.tensor.transpose(by_channel[:, b * P : (b + 1) * P], normed[p][:, b, :], identity[:])
+            result = work.tile([P, PIECE], F32, name="result")
+            nc.vector.scalar_tensor_tensor(result[:], by_channel[:], gamma_col, x_beta[:, pieces[p]], ALU.mult, ALU.add)
+            nc.sync.dma_start(out[:, pieces[p]], result[:])

@@ -54,6 +54,8 @@ def tile_graphtransformer_kernel(tc, x, wv, bv, wskip, bskip, gamma, beta, offs,
         make_identity(nc, identity[:])
         eps = held.tile([P, 1], F32, name="eps")
         nc.vector.memset(eps[:], EPS)
+        unread_rstd = held.tile([P, 1], F32, name="unread_rstd")
+        nc.scalar.activation(unread_rstd[:], eps[:], ACT.Abs_reciprocal_sqrt)
 
         columns_ps = psum.tile([P, P], F32, name="columns_ps", tag="bank")
         nc.tensor.transpose(columns_ps[:], rows[:], identity[:])

@@ -32,23 +32,23 @@ def tile_graphtransformer_kernel(tc, x, wv, bv, wskip, bskip, gamma, beta, offs,
         for w in range(WARM_UP):
             nc.tensor.matmul(unread_ps[:], zeros[:, 0:P], zeros[:], start=True, stop=True)
 
-        rows = held.tile([P, P], F32, name="rows")
-        nc.gpsimd.memset(rows[:], 0.0)
-        nc.sync.dma_start(rows[0:2, :], bv.rearrange("(h c) o -> (h o) c", h=HEADS))
-        nc.scalar.dma_start(rows[2:3, :], bskip.rearrange("c o -> o c"))
-        nc.sync.dma_start(rows[3:4, :], gamma.rearrange("c o -> o c"))
-        nc.scalar.dma_start(rows[4:5, :], beta.rearrange("c o -> o c"))
-
         offsets = held.tile([P, NODES // 16], U16, name="offsets")
         wv_sb = held.tile([P, HEADS * P], BF16, name="wv_sb")
         wskip_sb = held.tile([P, P], BF16, name="wskip_sb")
         x_sb = held.tile([P, NODES], BF16, name="x_sb")
-        nc.sync.dma_start(offsets[:], offs)
-        nc.scalar.dma_start(wskip_sb[:], wskip)
-        nc.scalar.dma_start(wv_sb[:], wv)
+        nc.sync.dma_start(wskip_sb[:], wskip)
         for p in range(PIECES):
-            queue = nc.sync if p % 2 == 0 else nc.scalar
+            queue = nc.scalar if p % 2 == 0 else nc.sync
             queue.dma_start(x_sb[:, pieces[p]], x[:, pieces[p]])
+        nc.scalar.dma_start(wv_sb[:], wv)
+        nc.sync.dma_start(offsets[:], offs)
+
+        columns = held.tile([P, 4, 8], F32, name="columns")
+        nc.sync.dma_start(columns[:, 0, 0:HEADS], bv.rearrange("(h c) o -> c (h o)", h=HEADS))
+        nc.scalar.dma_start(columns[:, 1, 0:1], bskip)
+        nc.gpsimd.dma_start(columns[:, 2, 0:1], beta)
+        nc.gpsimd.dma_start(columns[:, 3, 0:1], gamma)
+        beta_col, gamma_col = columns[:, 2, 0:1], columns[:, 3, 0:1]
 
         identity = held.tile([P, P], F32, name="identity")
         make_identity(nc, identity[:])
@@ -57,15 +57,10 @@ def tile_graphtransformer_kernel(tc, x, wv, bv, wskip, bskip, gamma, beta, offs,
         unread_rstd = held.tile([P, 1], F32, name="unread_rstd")
         nc.scalar.activation(unread_rstd[:], eps[:], ACT.Abs_reciprocal_sqrt)
 
-        columns_ps = psum.tile([P, P], F32, name="columns_ps", tag="bank")
-        nc.tensor.transpose(columns_ps[:], rows[:], identity[:])
-        columns = held.tile([P, 5], F32, name="columns")
-        nc.vector.tensor_copy(columns[:], columns_ps[:, 0:5])
-        gamma_col, beta_col = columns[:, 3:4], columns[:, 4:5]
         bv_sum = held.tile([P, 1], F32, name="bv_sum")
-        nc.vector.tensor_tensor(bv_sum[:], columns[:, 0:1], columns[:, 1:2], ALU.add)
+        nc.vector.tensor_tensor(bv_sum[:], columns[:, 0, 0:1], columns[:, 0, 1:2], ALU.add)
         bias = held.tile([P, 1], F32, name="bias")
-        nc.vector.scalar_tensor_tensor(bias[:], bv_sum[:], 0.5, columns[:, 2:3], ALU.mult, ALU.add)
+        nc.vector.scalar_tensor_tensor(bias[:], bv_sum[:], 0.5, columns[:, 1, 0:1], ALU.mult, ALU.add)
 
         wv_half = held.tile([P, HEADS * P], BF16, name="wv_half")
         nc.vector.tensor_scalar(wv_half[:], wv_sb[:], 0.5, None, ALU.mult)

@@ -10,7 +10,8 @@ HEADS = 2
 NODES = 2048
 PIECE = 512
 PIECES = NODES // PIECE
-BLOCKS = PIECE // P
+PAIR = 2 * P
+PAIRS = NODES // PAIR
 PSUM_BANKS = 8
 WARM_UP = 3
 EPS = 1e-5
@@ -23,7 +24,7 @@ def tile_graphtransformer_kernel(tc, x, wv, bv, wskip, bskip, gamma, beta, offs,
     pieces = [slice(p * PIECE, (p + 1) * PIECE) for p in range(PIECES)]
     with (
         tc.tile_pool(name="held", bufs=1) as held,
-        tc.tile_pool(name="work", bufs=PIECES) as work,
+        tc.tile_pool(name="work", bufs=PAIRS) as work,
         tc.psum_pool(name="psum", bufs=PSUM_BANKS) as psum,
     ):
         zeros = held.tile([P, PIECE], BF16, name="zeros")
@@ -79,36 +80,34 @@ def tile_graphtransformer_kernel(tc, x, wv, bv, wskip, bskip, gamma, beta, offs,
             nc.gpsimd.tensor_scalar(x_beta[:, pieces[p]], x_sb[:, pieces[p]], 1.0, beta_col, ALU.mult, ALU.add)
 
         by_node = []
-        for p in range(PIECES):
-            t = work.tile([P, PIECE], F32, name="t")
-            nc.scalar.activation(t[:], t_ps[p][:], ACT.Identity, bias=bias[:])
-            by_node.append(psum.tile([P, BLOCKS, P], F32, name="by_node", tag="bank"))
-            for b in range(BLOCKS):
-                nc.tensor.transpose(by_node[p][:, b, :], t[:, b * P : (b + 1) * P], identity[:])
+        for u in range(PAIRS):
+            t = work.tile([P, PAIR], F32, name="t")
+            half = slice((u % 2) * PAIR, (u % 2 + 1) * PAIR)
+            nc.scalar.activation(t[:], t_ps[u // 2][:, half], ACT.Identity, bias=bias[:])
+            by_node.append(psum.tile([P, 2, P], F32, name="by_node", tag="bank"))
+            for b in range(2):
+                nc.tensor.transpose(by_node[u][:, b, :], t[:, b * P : (b + 1) * P], identity[:])
 
         normed = []
-        for p in range(PIECES):
-            stats = work.tile([P, BLOCKS, 3], F32, name="stats")
-            for b in range(0, BLOCKS, 2):
-                nc.vector.bn_stats(
-                    stats[:, b : b + 2, :].rearrange("j b s -> j (b s)"),
-                    by_node[p][:, b : b + 2, :].rearrange("j b c -> j c b"),
-                )
+        for u in range(PAIRS):
+            stats = work.tile([P, 2, 3], F32, name="stats")
+            nc.vector.bn_stats(stats[:].rearrange("j b s -> j (b s)"), by_node[u][:].rearrange("j b c -> j c b"))
             mean, var_times_p = stats[:, :, 1], stats[:, :, 2]
-            rstd = work.tile([P, BLOCKS], F32, name="rstd")
+            rstd = work.tile([P, 2], F32, name="rstd")
             nc.scalar.activation(rstd[:], var_times_p, ACT.Abs_reciprocal_sqrt, bias=eps[:], scale=1.0 / P)
-            shift = work.tile([P, BLOCKS], F32, name="shift")
+            shift = work.tile([P, 2], F32, name="shift")
             nc.vector.scalar_tensor_tensor(shift[:], mean, -1.0, rstd[:], ALU.mult, ALU.mult)
-            normed.append(work.tile([P, BLOCKS, P], F32, name="normed"))
-            for b in range(BLOCKS):
+            normed.append(work.tile([P, 2, P], F32, name="normed"))
+            for b in range(2):
                 nc.scalar.activation(
-                    normed[p][:, b, :], by_node[p][:, b, :], ACT.Identity, bias=shift[:, b : b + 1], scale=rstd[:, b : b + 1]
+                    normed[u][:, b, :], by_node[u][:, b, :], ACT.Identity, bias=shift[:, b : b + 1], scale=rstd[:, b : b + 1]
                 )
 
-        for p in range(PIECES):
-            by_channel = psum.tile([P, PIECE], F32, name="by_channel", tag="bank")
-            for b in range(BLOCKS):
-                nc.tensor.transpose(by_channel[:, b * P : (b + 1) * P], normed[p][:, b, :], identity[:])
-            result = work.tile([P, PIECE], F32, name="result")
-            nc.vector.scalar_tensor_tensor(result[:], by_channel[:], gamma_col, x_beta[:, pieces[p]], ALU.mult, ALU.add)
-            nc.sync.dma_start(out[:, pieces[p]], result[:])
+        for u in range(PAIRS):
+            nodes = slice(u * PAIR, (u + 1) * PAIR)
+            by_channel = psum.tile([P, PAIR], F32, name="by_channel", tag="bank")
+            for b in range(2):
+                nc.tensor.transpose(by_channel[:, b * P : (b + 1) * P], normed[u][:, b, :], identity[:])
+            result = work.tile([P, PAIR], F32, name="result")
+            nc.vector.scalar_tensor_tensor(result[:], by_channel[:], gamma_col, x_beta[:, nodes], ALU.mult, ALU.add)
+            nc.sync.dma_start(out[:, nodes], result[:])

@@ -47,8 +47,8 @@ def tile_graphtransformer_kernel(tc, x, wv, bv, wskip, bskip, gamma, beta, offs,
         columns = held.tile([P, 4, 8], F32, name="columns")
         nc.sync.dma_start(columns[:, 0, 0:HEADS], bv.rearrange("(h c) o -> c (h o)", h=HEADS))
         nc.scalar.dma_start(columns[:, 1, 0:1], bskip)
-        nc.gpsimd.dma_start(columns[:, 2, 0:1], beta)
-        nc.gpsimd.dma_start(columns[:, 3, 0:1], gamma)
+        nc.sync.dma_start(columns[:, 2, 0:1], beta)
+        nc.sync.dma_start(columns[:, 3, 0:1], gamma)
         beta_col, gamma_col = columns[:, 2, 0:1], columns[:, 3, 0:1]
 
         identity = held.tile([P, P], F32, name="identity")

@@ -54,26 +54,26 @@ def tile_graphtransformer_kernel(tc, x, wv, bv, wskip, bskip, gamma, beta, offs,
         identity = held.tile([P, P], F32, name="identity")
         make_identity(nc, identity[:])
         eps = held.tile([P, 1], F32, name="eps")
-        nc.vector.memset(eps[:], EPS)
+        nc.vector.memset(eps[:], 4 * EPS)
         unread_rstd = held.tile([P, 1], F32, name="unread_rstd")
         nc.scalar.activation(unread_rstd[:], eps[:], ACT.Abs_reciprocal_sqrt)
+
+        wskip_twice = held.tile([P, P], BF16, name="wskip_twice")
+        nc.vector.tensor_scalar(wskip_twice[:], wskip_sb[:], 2.0, None, ALU.mult)
 
         bv_sum = held.tile([P, 1], F32, name="bv_sum")
         nc.vector.tensor_tensor(bv_sum[:], columns[:, 0, 0:1], columns[:, 0, 1:2], ALU.add)
         bias = held.tile([P, 1], F32, name="bias")
-        nc.vector.scalar_tensor_tensor(bias[:], bv_sum[:], 0.5, columns[:, 1, 0:1], ALU.mult, ALU.add)
-
-        wv_half = held.tile([P, HEADS * P], BF16, name="wv_half")
-        nc.vector.tensor_scalar(wv_half[:], wv_sb[:], 0.5, None, ALU.mult)
+        nc.vector.scalar_tensor_tensor(bias[:], columns[:, 1, 0:1], 2.0, bv_sum[:], ALU.mult, ALU.add)
 
         t_ps = [psum.tile([P, PIECE], F32, name="t_ps", tag="bank") for p in range(PIECES)]
         for p in range(PIECES):
-            nc.tensor.matmul(t_ps[p][:], wskip_sb[:], x_sb[:, pieces[p]], start=True, stop=False)
+            nc.tensor.matmul(t_ps[p][:], wskip_twice[:], x_sb[:, pieces[p]], start=True, stop=False)
 
         for p in range(PIECES):
             picked = x_sb[:].indirect(offsets[:, p * (PIECE // 16) : (p + 1) * (PIECE // 16)])
-            nc.tensor.matmul(t_ps[p][:], wv_half[:, 0:P], picked, start=False, stop=False)
-            nc.tensor.matmul(t_ps[p][:], wv_half[:, P : 2 * P], picked, start=False, stop=True)
+            nc.tensor.matmul(t_ps[p][:], wv_sb[:, 0:P], picked, start=False, stop=False)
+            nc.tensor.matmul(t_ps[p][:], wv_sb[:, P : 2 * P], picked, start=False, stop=True)
 
         x_beta = held.tile([P, NODES], F32, name="x_beta")
         for p in range(PIECES):

import concourse.mybir as mybir
from concourse.masks import make_identity

BF16, F32, U16 = mybir.dt.bfloat16, mybir.dt.float32, mybir.dt.uint16
ACT = mybir.ActivationFunctionType
ALU = mybir.AluOpType

P = 128
HEADS = 2
NODES = 2048
PIECE = 512
PIECES = NODES // PIECE
PAIR = 2 * P
PAIRS = NODES // PAIR
PSUM_BANKS = 8
WARM_UP = 3
EPS = 1e-5

FLOPS = 2 * P * (HEADS * P + P) * NODES


def tile_graphtransformer_kernel(tc, x, wv, bv, wskip, bskip, gamma, beta, offs, out):
    nc = tc.nc
    pieces = [slice(p * PIECE, (p + 1) * PIECE) for p in range(PIECES)]
    with (
        tc.tile_pool(name="held", bufs=1) as held,
        tc.tile_pool(name="work", bufs=PAIRS) as work,
        tc.psum_pool(name="psum", bufs=PSUM_BANKS) as psum,
    ):
        zeros = held.tile([P, PIECE], BF16, name="zeros")
        nc.vector.memset(zeros[:], 0.0)
        unread_ps = psum.tile([P, PIECE], F32, name="unread_ps", tag="bank")
        for w in range(WARM_UP):
            nc.tensor.matmul(unread_ps[:], zeros[:, 0:P], zeros[:], start=True, stop=True)

        offsets = held.tile([P, NODES // 16], U16, name="offsets")
        wv_sb = held.tile([P, HEADS * P], BF16, name="wv_sb")
        wskip_sb = held.tile([P, P], BF16, name="wskip_sb")
        x_sb = held.tile([P, NODES], BF16, name="x_sb")
        nc.sync.dma_start(wskip_sb[:], wskip)
        for p in range(PIECES):
            queue = nc.scalar if p % 2 == 0 else nc.sync
            queue.dma_start(x_sb[:, pieces[p]], x[:, pieces[p]])
        nc.scalar.dma_start(wv_sb[:], wv)
        nc.sync.dma_start(offsets[:], offs)

        columns = held.tile([P, 4, 8], F32, name="columns")
        nc.sync.dma_start(columns[:, 0, 0:HEADS], bv.rearrange("(h c) o -> c (h o)", h=HEADS))
        nc.scalar.dma_start(columns[:, 1, 0:1], bskip)
        nc.sync.dma_start(columns[:, 2, 0:1], beta)
        nc.sync.dma_start(columns[:, 3, 0:1], gamma)
        beta_col, gamma_col = columns[:, 2, 0:1], columns[:, 3, 0:1]

        identity = held.tile([P, P], F32, name="identity")
        make_identity(nc, identity[:])
        eps = held.tile([P, 1], F32, name="eps")
        nc.vector.memset(eps[:], 4 * EPS)
        unread_rstd = held.tile([P, 1], F32, name="unread_rstd")
        nc.scalar.activation(unread_rstd[:], eps[:], ACT.Abs_reciprocal_sqrt)

        wskip_twice = held.tile([P, P], BF16, name="wskip_twice")
        nc.vector.tensor_scalar(wskip_twice[:], wskip_sb[:], 2.0, None, ALU.mult)

        bv_sum = held.tile([P, 1], F32, name="bv_sum")
        nc.vector.tensor_tensor(bv_sum[:], columns[:, 0, 0:1], columns[:, 0, 1:2], ALU.add)
        bias = held.tile([P, 1], F32, name="bias")
        nc.vector.scalar_tensor_tensor(bias[:], columns[:, 1, 0:1], 2.0, bv_sum[:], ALU.mult, ALU.add)

        t_ps = [psum.tile([P, PIECE], F32, name="t_ps", tag="bank") for p in range(PIECES)]
        for p in range(PIECES):
            nc.tensor.matmul(t_ps[p][:], wskip_twice[:], x_sb[:, pieces[p]], start=True, stop=False)

        for p in range(PIECES):
            picked = x_sb[:].indirect(offsets[:, p * (PIECE // 16) : (p + 1) * (PIECE // 16)])
            nc.tensor.matmul(t_ps[p][:], wv_sb[:, 0:P], picked, start=False, stop=False)
            nc.tensor.matmul(t_ps[p][:], wv_sb[:, P : 2 * P], picked, start=False, stop=True)

        x_beta = held.tile([P, NODES], F32, name="x_beta")
        for p in range(PIECES):
            nc.gpsimd.tensor_scalar(x_beta[:, pieces[p]], x_sb[:, pieces[p]], 1.0, beta_col, ALU.mult, ALU.add)

        by_node = []
        for u in range(PAIRS):
            t = work.tile([P, PAIR], F32, name="t")
            half = slice((u % 2) * PAIR, (u % 2 + 1) * PAIR)
            nc.scalar.activation(t[:], t_ps[u // 2][:, half], ACT.Identity, bias=bias[:])
            by_node.append(psum.tile([P, 2, P], F32, name="by_node", tag="bank"))
            for b in range(2):
                nc.tensor.transpose(by_node[u][:, b, :], t[:, b * P : (b + 1) * P], identity[:])

        normed = []
        for u in range(PAIRS):
            stats = work.tile([P, 2, 3], F32, name="stats")
            nc.vector.bn_stats(stats[:].rearrange("j b s -> j (b s)"), by_node[u][:].rearrange("j b c -> j c b"))
            mean, var_times_p = stats[:, :, 1], stats[:, :, 2]
            rstd = work.tile([P, 2], F32, name="rstd")
            nc.scalar.activation(rstd[:], var_times_p, ACT.Abs_reciprocal_sqrt, bias=eps[:], scale=1.0 / P)
            shift = work.tile([P, 2], F32, name="shift")
            nc.vector.scalar_tensor_tensor(shift[:], mean, -1.0, rstd[:], ALU.mult, ALU.mult)
            normed.append(work.tile([P, 2, P], F32, name="normed"))
            for b in range(2):
                nc.scalar.activation(
                    normed[u][:, b, :], by_node[u][:, b, :], ACT.Identity, bias=shift[:, b : b + 1], scale=rstd[:, b : b + 1]
                )

        for u in range(PAIRS):
            nodes = slice(u * PAIR, (u + 1) * PAIR)
            by_channel = psum.tile([P, PAIR], F32, name="by_channel", tag="bank")
            for b in range(2):
                nc.tensor.transpose(by_channel[:, b * P : (b + 1) * P], normed[u][:, b, :], identity[:])
            result = work.tile([P, PAIR], F32, name="result")
            nc.vector.scalar_tensor_tensor(result[:], by_channel[:], gamma_col, x_beta[:, nodes], ALU.mult, ALU.add)
            nc.sync.dma_start(out[:, nodes], result[:])
